import numpy as np
import ml_dtypes


def mxq(x, axis, fmt="e4m3"):
    dtype, down = {"e4m3": (ml_dtypes.float8_e4m3fn, 7), "e5m2": (ml_dtypes.float8_e5m2, 14)}[fmt]
    v = np.moveaxis(np.asarray(x, np.float32).astype(ml_dtypes.bfloat16).astype(np.float64), axis, -1)
    blocks = v.reshape(v.shape[:-1] + (-1, 32))
    amax = np.abs(blocks).max(-1, keepdims=True)
    byte = np.maximum(np.where(amax > 0, np.frexp(amax)[1] - 1 + 127, 0) - down, 1)
    scale = np.exp2(byte - 127.0)
    codes = (blocks / scale).astype(np.float32).astype(dtype).astype(np.float64)
    return np.moveaxis((codes * scale).reshape(v.shape), -1, axis)


WIDE = False


def mx_kscale(k):
    if not WIDE:
        return np.ones(k)
    levels = np.array([10, -10, 5, -5, 0])
    a = np.random.permutation(np.resize(levels, k // 512 * 4)).reshape(k // 512, 4)
    idx = np.arange(k)
    return np.exp2(a[idx // 512, idx % 128 // 32])


BF16 = ml_dtypes.bfloat16


def bf(x):
    return np.asarray(x, np.float32).astype(BF16)


def f64(x):
    return np.asarray(x).astype(np.float64)


B, C, HH, WW, NH = 4, 512, 32, 32, 8
N = HH * WW
DH = C // NH
HALF = C // 2


def pos_encoding():
    positions = np.arange(N, dtype=np.float64)
    depths = np.arange(HALF, dtype=np.float64) / HALF
    angle_rates = 1.0 / (10000.0 ** depths)
    angle_rads = positions[:, None] * angle_rates[None, :]
    return np.concatenate([np.sin(angle_rads), np.cos(angle_rads)], axis=-1)


def heads(t):
    return t.reshape(B, N, NH, DH).transpose(0, 2, 1, 3)


def setup_inputs():
    bound = np.sqrt(6.0 / (C + 3 * C))
    s = mx_kscale(C)
    u = s / s.min()
    return {"x": bf(np.random.standard_normal((B, C, HH, WW)) * u[None, :, None, None]),
            "W_qkv": bf(np.random.uniform(-bound, bound, (3 * C, C)) / u[None, :])}


def reference(x, W_qkv):
    xt = f64(x).reshape(B, C, N) + pos_encoding().T[None]
    tokens = xt.transpose(0, 2, 1)
    qkv = mxq(tokens, 2, "e4m3") @ mxq(f64(W_qkv), 1, "e4m3").T
    q, k, v = np.split(qkv, 3, axis=-1)
    return heads(q), heads(k), heads(v)

@@ -1,0 +1,235 @@
+import math
+from contextlib import ExitStack
+
+import concourse.mybir as mybir
+from concourse.masks import make_identity
+
+F32 = mybir.dt.float32
+BF16 = mybir.dt.bfloat16
+U32 = mybir.dt.uint32
+U8 = mybir.dt.uint8
+FP8X4 = mybir.dt.float8_e4m3fn_x4
+ALU = mybir.AluOpType
+ACT = mybir.ActivationFunctionType
+
+P = 128
+PACK = 4
+BATCH = 4
+CHANNELS = 512
+POSITIONS = 1024
+HEADS = 8
+HEAD_DIM = 64
+OUT_COLS = HEADS * HEAD_DIM
+RUN = 8
+HALF_RUN = RUN // 2
+GROUPS = POSITIONS // RUN
+HALF_COLS = GROUPS * HALF_RUN
+ROUND_MAGIC = 12582912.0
+
+FLOPS = 2 * BATCH * POSITIONS * CHANNELS * 3 * OUT_COLS
+
+
+def tile_multiheadselfattention_pa_t_kernel(tc, x, W_qkv, out_0, out_1, out_2):
+    nc = tc.nc
+    outs = [out_0, out_1, out_2]
+    with ExitStack() as ctx:
+        const = ctx.enter_context(tc.tile_pool(name="const", bufs=1))
+        angles = ctx.enter_context(tc.tile_pool(name="angles", bufs=2))
+        tokens = ctx.enter_context(tc.tile_pool(name="tokens", bufs=2))
+        staging = ctx.enter_context(tc.tile_pool(name="staging", bufs=5))
+        psum_w = ctx.enter_context(tc.psum_pool(name="psum_w", bufs=2))
+        psum_o = ctx.enter_context(tc.psum_pool(name="psum_o", bufs=6))
+
+        w_raw = const.tile([P, 12, CHANNELS], BF16)
+        x_raw = [const.tile([P, PACK, POSITIONS], BF16, name="x_raw%d" % b) for b in range(BATCH)]
+
+        def load_w(g):
+            nc.sync.dma_start(
+                out=w_raw[:, 4 * g : 4 * g + 4, :],
+                in_=W_qkv[OUT_COLS * g : OUT_COLS * (g + 1), :].rearrange("(a o) k -> o a k", o=P),
+            )
+
+        def load_x(b):
+            nc.sync.dma_start(
+                out=x_raw[b][:].rearrange("q (u e) n -> q u e n", u=2),
+                in_=x[b].rearrange("c h w -> c (h w)").rearrange("(u q e) n -> q u e n", u=2, e=2),
+            )
+
+        load_w(0)
+        load_x(0)
+        load_w(1)
+        load_w(2)
+        for b in range(1, BATCH):
+            load_x(b)
+
+        zero = const.tile([P, 1], F32)
+        nc.vector.memset(zero[:], 0.0)
+        warm = const.tile([P, 1], F32)
+        nc.scalar.activation(out=warm[:], in_=zero[:], func=ACT.Sin)
+        half_pi = const.tile([P, 1], F32)
+        nc.vector.tensor_scalar(
+            out=half_pi[:], in0=zero[:], scalar1=math.pi / 2, scalar2=None, op0=ALU.add
+        )
+
+        rate_index = const.tile([P, 2], F32)
+        nc.gpsimd.iota(
+            rate_index[:],
+            pattern=[[1, 2]],
+            base=0,
+            channel_multiplier=2,
+            allow_small_or_imprecise_dtypes=True,
+        )
+        ten_thousand = const.tile([P, 2], F32)
+        nc.gpsimd.memset(ten_thousand[:], 10000.0)
+        exponent = const.tile([P, 2], F32)
+        nc.gpsimd.tensor_scalar(
+            out=exponent[:], in0=rate_index[:], scalar1=-1.0 / 256.0, scalar2=0.0,
+            op0=ALU.mult, op1=ALU.add,
+        )
+        rate = const.tile([P, 2], F32)
+        nc.gpsimd.tensor_tensor(out=rate[:], in0=ten_thousand[:], in1=exponent[:], op=ALU.pow)
+        turns = const.tile([P, 2], F32)
+        nc.gpsimd.tensor_scalar(
+            out=turns[:], in0=rate[:], scalar1=1.0 / (2.0 * math.pi), scalar2=0.0,
+            op0=ALU.mult, op1=ALU.add,
+        )
+
+        position = const.tile([P, 2, HALF_COLS], F32)
+        nc.gpsimd.iota(
+            position[:, 0, :],
+            pattern=[[RUN, GROUPS], [1, HALF_RUN]],
+            base=0,
+            channel_multiplier=0,
+            allow_small_or_imprecise_dtypes=True,
+        )
+        nc.vector.tensor_scalar(
+            out=position[:, 1, :], in0=position[:, 0, :], scalar1=float(HALF_RUN), scalar2=None,
+            op0=ALU.add,
+        )
+
+        identity = const.tile([P, P], F32)
+        make_identity(nc, identity[:])
+
+        w_grouped = const.tile([P, 3 * OUT_COLS * PACK], BF16, align_bytes=64)
+        w_words = w_grouped[:].bitcast(F32).rearrange("q (o u) -> q o u", u=2)
+        w_codes = const.tile([P, 3 * OUT_COLS], U32, align_bytes=64)
+        w_scales = const.tile([P, 3 * OUT_COLS], U8, align_bytes=64)
+
+        def prepare_w(g):
+            for pair in range(2 * g, 2 * g + 2):
+                flipped = psum_w.tile([P, 2, 2, P], F32)
+                for a in range(2):
+                    words = w_raw[:, 2 * pair + a, :].bitcast(F32)
+                    for u in range(2):
+                        nc.tensor.transpose(
+                            flipped[:, a, u, :], words[:, P * u : P * (u + 1)], identity[:]
+                        )
+                nc.scalar.copy(
+                    out=w_words[:, 2 * P * pair : 2 * P * (pair + 1), :].rearrange(
+                        "q (a o) u -> q a o u", a=2
+                    ),
+                    in_=flipped[:].rearrange("q a u o -> q a o u"),
+                )
+            cols = slice(OUT_COLS * g, OUT_COLS * (g + 1))
+            nc.vector.quantize_mx(
+                out=w_codes[:, cols].bitcast(FP8X4),
+                scales=w_scales[:, cols],
+                in_=w_grouped[:, PACK * OUT_COLS * g : PACK * OUT_COLS * (g + 1)],
+            )
+
+        pe = [const.tile([P, PACK, HALF_COLS], F32, name="pe%d" % s) for s in range(2)]
+
+        def make_table(s, e):
+            angle = angles.tile([P, HALF_COLS], F32)
+            nc.vector.tensor_scalar(
+                out=angle[:], in0=position[:, s, :], scalar1=turns[:, e : e + 1], scalar2=None,
+                op0=ALU.mult,
+            )
+            whole = angles.tile([P, HALF_COLS], F32)
+            nc.vector.tensor_scalar(
+                out=whole[:], in0=angle[:], scalar1=ROUND_MAGIC, scalar2=None, op0=ALU.add
+            )
+            back = angles.tile([P, HALF_COLS], F32)
+            nc.vector.scalar_tensor_tensor(
+                out=back[:], in0=whole[:], scalar=ROUND_MAGIC, in1=angle[:],
+                op0=ALU.subtract, op1=ALU.subtract,
+            )
+            nc.scalar.activation(out=pe[s][:, e, :], in_=back[:], func=ACT.Sin, scale=-2.0 * math.pi)
+            size = angles.tile([P, HALF_COLS], F32)
+            nc.scalar.activation(out=size[:], in_=back[:], func=ACT.Abs)
+            nc.scalar.activation(
+                out=pe[s][:, 2 + e, :], in_=size[:], func=ACT.Sin, scale=-2.0 * math.pi,
+                bias=half_pi[:],
+            )
+
+        token_tiles = {}
+
+        def add_table(b, s):
+            if s == 0:
+                token_tiles[b] = (
+                    tokens.tile([P, RUN, GROUPS, PACK], BF16, name="grouped", align_bytes=64),
+                    tokens.tile([P, RUN, GROUPS], U32, name="codes", align_bytes=64),
+                    tokens.tile([P, RUN, GROUPS], U8, name="scales", align_bytes=64),
+                )
+            grouped = token_tiles[b][0]
+            half = slice(HALF_RUN * s, HALF_RUN * (s + 1))
+            nc.vector.tensor_tensor(
+                out=grouped[:, half, :, :].rearrange("q t m j -> q m j t"),
+                in0=x_raw[b][:].rearrange("q j (m s t) -> q s m j t", s=2, t=HALF_RUN)[:, s],
+                in1=pe[s][:].rearrange("q j (m t) -> q m j t", t=HALF_RUN),
+                op=ALU.add,
+            )
+
+        def quantise_tokens(b, s):
+            grouped, codes, scales = token_tiles[b]
+            half = slice(HALF_RUN * s, HALF_RUN * (s + 1))
+            nc.vector.quantize_mx(
+                out=codes[:, half, :].rearrange("q t m -> q (t m)").bitcast(FP8X4),
+                scales=scales[:, half, :].rearrange("q t m -> q (t m)"),
+                in_=grouped[:, half, :, :].rearrange("q t m j -> q (t m j)"),
+            )
+
+        def prepare_tokens(b, step):
+            if step < 2:
+                add_table(b, step)
+            if step > 0:
+                quantise_tokens(b, step - 1)
+
+        def project(b, g):
+            codes, scales = token_tiles[b][1], token_tiles[b][2]
+            cols = slice(OUT_COLS * g, OUT_COLS * (g + 1))
+            stage = staging.tile([P, HEADS, RUN, HEAD_DIM], F32)
+            for t in range(RUN):
+                acc = psum_o.tile([P, OUT_COLS], F32)
+                nc.tensor.matmul_mx(
+                    out=acc[:],
+                    lhsT=codes[:, t, :].bitcast(FP8X4),
+                    lhsT_scale=scales[:, t, :],
+                    rhs=w_codes[:, cols].bitcast(FP8X4),
+                    rhs_scale=w_scales[:, cols],
+                    start=True,
+                    stop=True,
+                )
+                by_head = acc[:].rearrange("m (h d) -> m h d", d=HEAD_DIM)
+                if t % 4 == 3:
+                    nc.vector.tensor_copy(out=stage[:, :, t, :], in_=by_head)
+                else:
+                    nc.scalar.copy(out=stage[:, :, t, :], in_=by_head)
+            nc.sync.dma_start(
+                out=outs[g][b].rearrange("h (m t) d -> m h (t d)", t=RUN),
+                in_=stage[:].rearrange("m h t d -> m h (t d)"),
+            )
+
+        prepare_w(0)
+        for s in range(2):
+            for e in range(2):
+                make_table(s, e)
+        for step in range(3):
+            prepare_tokens(0, step)
+        prepare_w(1)
+        prepare_w(2)
+        for b in range(BATCH):
+            for g in range(3):
+                project(b, g)
+                if b + 1 < BATCH:
+                    prepare_tokens(b + 1, g)

@@ -34,11 +34,12 @@ def tile_multiheadselfattention_pa_t_kernel(tc, x, W_qkv, out_0, out_1, out_2):
     outs = [out_0, out_1, out_2]
     with ExitStack() as ctx:
         const = ctx.enter_context(tc.tile_pool(name="const", bufs=1))
-        angles = ctx.enter_context(tc.tile_pool(name="angles", bufs=2))
+        angles = ctx.enter_context(tc.tile_pool(name="angles", bufs=4))
         tokens = ctx.enter_context(tc.tile_pool(name="tokens", bufs=2))
         staging = ctx.enter_context(tc.tile_pool(name="staging", bufs=5))
-        psum_w = ctx.enter_context(tc.psum_pool(name="psum_w", bufs=2))
-        psum_o = ctx.enter_context(tc.psum_pool(name="psum_o", bufs=6))
+        psum_w = ctx.enter_context(tc.psum_pool(name="psum_w", bufs=4))
+        psum_o = ctx.enter_context(tc.psum_pool(name="psum_o", bufs=4))
+        ctx.enter_context(tc.manual_schedule())
 
         w_raw = const.tile([P, 12, CHANNELS], BF16)
         x_raw = [const.tile([P, PACK, POSITIONS], BF16, name="x_raw%d" % b) for b in range(BATCH)]
@@ -64,6 +65,8 @@ def tile_multiheadselfattention_pa_t_kernel(tc, x, W_qkv, out_0, out_1, out_2):
 
         zero = const.tile([P, 1], F32)
         nc.vector.memset(zero[:], 0.0)
+        ten_thousand = const.tile([P, 2], F32)
+        nc.vector.memset(ten_thousand[:], 10000.0)
         warm = const.tile([P, 1], F32)
         nc.scalar.activation(out=warm[:], in_=zero[:], func=ACT.Sin)
         half_pi = const.tile([P, 1], F32)
@@ -71,16 +74,32 @@ def tile_multiheadselfattention_pa_t_kernel(tc, x, W_qkv, out_0, out_1, out_2):
             out=half_pi[:], in0=zero[:], scalar1=math.pi / 2, scalar2=None, op0=ALU.add
         )
 
-        rate_index = const.tile([P, 2], F32)
+        run_start = const.tile([P, GROUPS], F32)
         nc.gpsimd.iota(
-            rate_index[:],
-            pattern=[[1, 2]],
-            base=0,
-            channel_multiplier=2,
+            run_start[:], pattern=[[RUN, GROUPS]], base=0, channel_multiplier=0,
             allow_small_or_imprecise_dtypes=True,
         )
-        ten_thousand = const.tile([P, 2], F32)
-        nc.gpsimd.memset(ten_thousand[:], 10000.0)
+        in_run = const.tile([P, RUN], F32)
+        nc.gpsimd.iota(
+            in_run[:], pattern=[[1, RUN]], base=0, channel_multiplier=0,
+            allow_small_or_imprecise_dtypes=True,
+        )
+        position = const.tile([P, 2, GROUPS, HALF_RUN], F32)
+        for s in range(2):
+            nc.vector.tensor_tensor(
+                out=position[:, s, :, :],
+                in0=run_start[:].unsqueeze(2).to_broadcast([P, GROUPS, HALF_RUN]),
+                in1=in_run[:, HALF_RUN * s : HALF_RUN * (s + 1)]
+                .unsqueeze(1)
+                .to_broadcast([P, GROUPS, HALF_RUN]),
+                op=ALU.add,
+            )
+
+        rate_index = const.tile([P, 2], F32)
+        nc.gpsimd.iota(
+            rate_index[:], pattern=[[1, 2]], base=0, channel_multiplier=2,
+            allow_small_or_imprecise_dtypes=True,
+        )
         exponent = const.tile([P, 2], F32)
         nc.gpsimd.tensor_scalar(
             out=exponent[:], in0=rate_index[:], scalar1=-1.0 / 256.0, scalar2=0.0,
@@ -94,19 +113,6 @@ def tile_multiheadselfattention_pa_t_kernel(tc, x, W_qkv, out_0, out_1, out_2):
             op0=ALU.mult, op1=ALU.add,
         )
 
-        position = const.tile([P, 2, HALF_COLS], F32)
-        nc.gpsimd.iota(
-            position[:, 0, :],
-            pattern=[[RUN, GROUPS], [1, HALF_RUN]],
-            base=0,
-            channel_multiplier=0,
-            allow_small_or_imprecise_dtypes=True,
-        )
-        nc.vector.tensor_scalar(
-            out=position[:, 1, :], in0=position[:, 0, :], scalar1=float(HALF_RUN), scalar2=None,
-            op0=ALU.add,
-        )
-
         identity = const.tile([P, P], F32)
         make_identity(nc, identity[:])
 
@@ -114,22 +120,30 @@ def tile_multiheadselfattention_pa_t_kernel(tc, x, W_qkv, out_0, out_1, out_2):
         w_words = w_grouped[:].bitcast(F32).rearrange("q (o u) -> q o u", u=2)
         w_codes = const.tile([P, 3 * OUT_COLS], U32, align_bytes=64)
         w_scales = const.tile([P, 3 * OUT_COLS], U8, align_bytes=64)
+        flipped = {}
 
-        def prepare_w(g):
+        def flip_w(g):
             for pair in range(2 * g, 2 * g + 2):
-                flipped = psum_w.tile([P, 2, 2, P], F32)
+                flipped[pair] = psum_w.tile([P, 2, 2, P], F32, name="flipped")
                 for a in range(2):
                     words = w_raw[:, 2 * pair + a, :].bitcast(F32)
                     for u in range(2):
                         nc.tensor.transpose(
-                            flipped[:, a, u, :], words[:, P * u : P * (u + 1)], identity[:]
+                            flipped[pair][:, a, u, :], words[:, P * u : P * (u + 1)], identity[:]
                         )
-                nc.scalar.copy(
-                    out=w_words[:, 2 * P * pair : 2 * P * (pair + 1), :].rearrange(
-                        "q (a o) u -> q a o u", a=2
-                    ),
-                    in_=flipped[:].rearrange("q a u o -> q a o u"),
+
+        def regroup_w(g):
+            for pair in range(2 * g, 2 * g + 2):
+                dst = w_words[:, 2 * P * pair : 2 * P * (pair + 1), :].rearrange(
+                    "q (a o) u -> q a o u", a=2
                 )
+                src = flipped[pair][:].rearrange("q a u o -> q a o u")
+                if g % 2 == 0:
+                    nc.scalar.copy(out=dst, in_=src)
+                else:
+                    nc.vector.tensor_copy(out=dst, in_=src)
+
+        def quantise_w(g):
             cols = slice(OUT_COLS * g, OUT_COLS * (g + 1))
             nc.vector.quantize_mx(
                 out=w_codes[:, cols].bitcast(FP8X4),
@@ -142,8 +156,8 @@ def tile_multiheadselfattention_pa_t_kernel(tc, x, W_qkv, out_0, out_1, out_2):
         def make_table(s, e):
             angle = angles.tile([P, HALF_COLS], F32)
             nc.vector.tensor_scalar(
-                out=angle[:], in0=position[:, s, :], scalar1=turns[:, e : e + 1], scalar2=None,
-                op0=ALU.mult,
+                out=angle[:], in0=position[:, s, :, :].rearrange("q m t -> q (m t)"),
+                scalar1=turns[:, e : e + 1], scalar2=None, op0=ALU.mult,
             )
             whole = angles.tile([P, HALF_COLS], F32)
             nc.vector.tensor_scalar(
@@ -195,11 +209,15 @@ def tile_multiheadselfattention_pa_t_kernel(tc, x, W_qkv, out_0, out_1, out_2):
             if step > 0:
                 quantise_tokens(b, step - 1)
 
-        def project(b, g):
+        stage_tiles = {}
+
+        def project(b, g, s):
             codes, scales = token_tiles[b][1], token_tiles[b][2]
             cols = slice(OUT_COLS * g, OUT_COLS * (g + 1))
-            stage = staging.tile([P, HEADS, RUN, HEAD_DIM], F32)
-            for t in range(RUN):
+            if s == 0:
+                stage_tiles[(b, g)] = staging.tile([P, HEADS, RUN, HEAD_DIM], F32, name="stage")
+            stage = stage_tiles[(b, g)]
+            for t in range(HALF_RUN * s, HALF_RUN * (s + 1)):
                 acc = psum_o.tile([P, OUT_COLS], F32)
                 nc.tensor.matmul_mx(
                     out=acc[:],
@@ -215,21 +233,44 @@ def tile_multiheadselfattention_pa_t_kernel(tc, x, W_qkv, out_0, out_1, out_2):
                     nc.vector.tensor_copy(out=stage[:, :, t, :], in_=by_head)
                 else:
                     nc.scalar.copy(out=stage[:, :, t, :], in_=by_head)
+
+        def store(b, g, part, parts):
             nc.sync.dma_start(
-                out=outs[g][b].rearrange("h (m t) d -> m h (t d)", t=RUN),
-                in_=stage[:].rearrange("m h t d -> m h (t d)"),
+                out=outs[g][b].rearrange("h (m c r) d -> c m h (r d)", c=parts, r=RUN // parts)[part],
+                in_=stage_tiles[(b, g)][:].rearrange("m h (c r) d -> m c h (r d)", c=parts)[:, part],
             )
 
-        prepare_w(0)
-        for s in range(2):
-            for e in range(2):
-                make_table(s, e)
-        for step in range(3):
-            prepare_tokens(0, step)
-        prepare_w(1)
-        prepare_w(2)
-        for b in range(BATCH):
+        make_table(0, 0)
+        make_table(0, 1)
+        flip_w(0)
+        flip_w(1)
+        regroup_w(0)
+        make_table(1, 0)
+        make_table(1, 1)
+        flip_w(2)
+        add_table(0, 0)
+        quantise_w(0)
+        quantise_tokens(0, 0)
+        regroup_w(1)
+        quantise_w(1)
+        project(0, 0, 0)
+        store(0, 0, 0, 2)
+        regroup_w(2)
+        add_table(0, 1)
+        quantise_w(2)
+        quantise_tokens(0, 1)
+        for g in range(1, 3):
+            project(0, g, 0)
+            store(0, g, 0, 2)
+        for g in range(3):
+            project(0, g, 1)
+            store(0, g, 1, 2)
+            prepare_tokens(1, g)
+
+        for b in range(1, BATCH):
             for g in range(3):
-                project(b, g)
+                project(b, g, 0)
+                project(b, g, 1)
+                store(b, g, 0, 1)
                 if b + 1 < BATCH:
                     prepare_tokens(b + 1, g)

@@ -20,6 +20,7 @@ POSITIONS = 1024
 HEADS = 8
 HEAD_DIM = 64
 OUT_COLS = HEADS * HEAD_DIM
+STORE_HEADS = 4
 RUN = 8
 HALF_RUN = RUN // 2
 GROUPS = POSITIONS // RUN
@@ -235,10 +236,16 @@ def tile_multiheadselfattention_pa_t_kernel(tc, x, W_qkv, out_0, out_1, out_2):
                     nc.scalar.copy(out=stage[:, :, t, :], in_=by_head)
 
         def store(b, g, part, parts):
-            nc.sync.dma_start(
-                out=outs[g][b].rearrange("h (m c r) d -> c m h (r d)", c=parts, r=RUN // parts)[part],
-                in_=stage_tiles[(b, g)][:].rearrange("m h (c r) d -> m c h (r d)", c=parts)[:, part],
-            )
+            for first in range(0, HEADS, STORE_HEADS):
+                some = slice(first, first + STORE_HEADS)
+                nc.sync.dma_start(
+                    out=outs[g][b][some].rearrange(
+                        "h (m c r) d -> c m h (r d)", c=parts, r=RUN // parts
+                    )[part],
+                    in_=stage_tiles[(b, g)][:, some].rearrange(
+                        "m h (c r) d -> m c h (r d)", c=parts
+                    )[:, part],
+                )
 
         make_table(0, 0)
         make_table(0, 1)

@@ -20,7 +20,6 @@ POSITIONS = 1024
 HEADS = 8
 HEAD_DIM = 64
 OUT_COLS = HEADS * HEAD_DIM
-STORE_HEADS = 4
 RUN = 8
 HALF_RUN = RUN // 2
 GROUPS = POSITIONS // RUN
@@ -38,8 +37,7 @@ def tile_multiheadselfattention_pa_t_kernel(tc, x, W_qkv, out_0, out_1, out_2):
         angles = ctx.enter_context(tc.tile_pool(name="angles", bufs=4))
         tokens = ctx.enter_context(tc.tile_pool(name="tokens", bufs=2))
         staging = ctx.enter_context(tc.tile_pool(name="staging", bufs=5))
-        psum_w = ctx.enter_context(tc.psum_pool(name="psum_w", bufs=4))
-        psum_o = ctx.enter_context(tc.psum_pool(name="psum_o", bufs=4))
+        psum = ctx.enter_context(tc.psum_pool(name="psum", bufs=8))
         ctx.enter_context(tc.manual_schedule())
 
         w_raw = const.tile([P, 12, CHANNELS], BF16)
@@ -75,25 +73,22 @@ def tile_multiheadselfattention_pa_t_kernel(tc, x, W_qkv, out_0, out_1, out_2):
             out=half_pi[:], in0=zero[:], scalar1=math.pi / 2, scalar2=None, op0=ALU.add
         )
 
-        run_start = const.tile([P, GROUPS], F32)
+        count = const.tile([P, GROUPS], F32)
         nc.gpsimd.iota(
-            run_start[:], pattern=[[RUN, GROUPS]], base=0, channel_multiplier=0,
-            allow_small_or_imprecise_dtypes=True,
-        )
-        in_run = const.tile([P, RUN], F32)
-        nc.gpsimd.iota(
-            in_run[:], pattern=[[1, RUN]], base=0, channel_multiplier=0,
+            count[:], pattern=[[1, GROUPS]], base=0, channel_multiplier=0,
             allow_small_or_imprecise_dtypes=True,
         )
         position = const.tile([P, 2, GROUPS, HALF_RUN], F32)
         for s in range(2):
-            nc.vector.tensor_tensor(
+            nc.vector.scalar_tensor_tensor(
                 out=position[:, s, :, :],
-                in0=run_start[:].unsqueeze(2).to_broadcast([P, GROUPS, HALF_RUN]),
-                in1=in_run[:, HALF_RUN * s : HALF_RUN * (s + 1)]
+                in0=count[:].unsqueeze(2).to_broadcast([P, GROUPS, HALF_RUN]),
+                scalar=float(RUN),
+                in1=count[:, HALF_RUN * s : HALF_RUN * (s + 1)]
                 .unsqueeze(1)
                 .to_broadcast([P, GROUPS, HALF_RUN]),
-                op=ALU.add,
+                op0=ALU.mult,
+                op1=ALU.add,
             )
 
         rate_index = const.tile([P, 2], F32)
@@ -108,11 +103,6 @@ def tile_multiheadselfattention_pa_t_kernel(tc, x, W_qkv, out_0, out_1, out_2):
         )
         rate = const.tile([P, 2], F32)
         nc.gpsimd.tensor_tensor(out=rate[:], in0=ten_thousand[:], in1=exponent[:], op=ALU.pow)
-        turns = const.tile([P, 2], F32)
-        nc.gpsimd.tensor_scalar(
-            out=turns[:], in0=rate[:], scalar1=1.0 / (2.0 * math.pi), scalar2=0.0,
-            op0=ALU.mult, op1=ALU.add,
-        )
 
         identity = const.tile([P, P], F32)
         make_identity(nc, identity[:])
@@ -125,7 +115,7 @@ def tile_multiheadselfattention_pa_t_kernel(tc, x, W_qkv, out_0, out_1, out_2):
 
         def flip_w(g):
             for pair in range(2 * g, 2 * g + 2):
-                flipped[pair] = psum_w.tile([P, 2, 2, P], F32, name="flipped")
+                flipped[pair] = psum.tile([P, 2, 2, P], F32, name="flipped", tag="bank")
                 for a in range(2):
                     words = w_raw[:, 2 * pair + a, :].bitcast(F32)
                     for u in range(2):
@@ -158,7 +148,7 @@ def tile_multiheadselfattention_pa_t_kernel(tc, x, W_qkv, out_0, out_1, out_2):
             angle = angles.tile([P, HALF_COLS], F32)
             nc.vector.tensor_scalar(
                 out=angle[:], in0=position[:, s, :, :].rearrange("q m t -> q (m t)"),
-                scalar1=turns[:, e : e + 1], scalar2=None, op0=ALU.mult,
+                scalar1=rate[:, e : e + 1], scalar2=1.0 / (2.0 * math.pi), op0=ALU.mult, op1=ALU.mult,
             )
             whole = angles.tile([P, HALF_COLS], F32)
             nc.vector.tensor_scalar(
@@ -169,9 +159,9 @@ def tile_multiheadselfattention_pa_t_kernel(tc, x, W_qkv, out_0, out_1, out_2):
                 out=back[:], in0=whole[:], scalar=ROUND_MAGIC, in1=angle[:],
                 op0=ALU.subtract, op1=ALU.subtract,
             )
-            nc.scalar.activation(out=pe[s][:, e, :], in_=back[:], func=ACT.Sin, scale=-2.0 * math.pi)
             size = angles.tile([P, HALF_COLS], F32)
             nc.scalar.activation(out=size[:], in_=back[:], func=ACT.Abs)
+            nc.scalar.activation(out=pe[s][:, e, :], in_=back[:], func=ACT.Sin, scale=-2.0 * math.pi)
             nc.scalar.activation(
                 out=pe[s][:, 2 + e, :], in_=size[:], func=ACT.Sin, scale=-2.0 * math.pi,
                 bias=half_pi[:],
@@ -219,7 +209,7 @@ def tile_multiheadselfattention_pa_t_kernel(tc, x, W_qkv, out_0, out_1, out_2):
                 stage_tiles[(b, g)] = staging.tile([P, HEADS, RUN, HEAD_DIM], F32, name="stage")
             stage = stage_tiles[(b, g)]
             for t in range(HALF_RUN * s, HALF_RUN * (s + 1)):
-                acc = psum_o.tile([P, OUT_COLS], F32)
+                acc = psum.tile([P, OUT_COLS], F32, tag="bank")
                 nc.tensor.matmul_mx(
                     out=acc[:],
                     lhsT=codes[:, t, :].bitcast(FP8X4),
@@ -236,16 +226,10 @@ def tile_multiheadselfattention_pa_t_kernel(tc, x, W_qkv, out_0, out_1, out_2):
                     nc.scalar.copy(out=stage[:, :, t, :], in_=by_head)
 
         def store(b, g, part, parts):
-            for first in range(0, HEADS, STORE_HEADS):
-                some = slice(first, first + STORE_HEADS)
-                nc.sync.dma_start(
-                    out=outs[g][b][some].rearrange(
-                        "h (m c r) d -> c m h (r d)", c=parts, r=RUN // parts
-                    )[part],
-                    in_=stage_tiles[(b, g)][:, some].rearrange(
-                        "m h (c r) d -> m c h (r d)", c=parts
-                    )[:, part],
-                )
+            nc.sync.dma_start(
+                out=outs[g][b].rearrange("h (m c r) d -> c m h (r d)", c=parts, r=RUN // parts)[part],
+                in_=stage_tiles[(b, g)][:].rearrange("m h (c r) d -> m c h (r d)", c=parts)[:, part],
+            )
 
         make_table(0, 0)
         make_table(0, 1)

import math
from contextlib import ExitStack

import concourse.mybir as mybir
from concourse.masks import make_identity

F32 = mybir.dt.float32
BF16 = mybir.dt.bfloat16
U32 = mybir.dt.uint32
U8 = mybir.dt.uint8
FP8X4 = mybir.dt.float8_e4m3fn_x4
ALU = mybir.AluOpType
ACT = mybir.ActivationFunctionType

P = 128
PACK = 4
BATCH = 4
CHANNELS = 512
POSITIONS = 1024
HEADS = 8
HEAD_DIM = 64
OUT_COLS = HEADS * HEAD_DIM
RUN = 8
HALF_RUN = RUN // 2
GROUPS = POSITIONS // RUN
HALF_COLS = GROUPS * HALF_RUN
ROUND_MAGIC = 12582912.0

FLOPS = 2 * BATCH * POSITIONS * CHANNELS * 3 * OUT_COLS


def tile_multiheadselfattention_pa_t_kernel(tc, x, W_qkv, out_0, out_1, out_2):
    nc = tc.nc
    outs = [out_0, out_1, out_2]
    with ExitStack() as ctx:
        const = ctx.enter_context(tc.tile_pool(name="const", bufs=1))
        angles = ctx.enter_context(tc.tile_pool(name="angles", bufs=4))
        tokens = ctx.enter_context(tc.tile_pool(name="tokens", bufs=2))
        staging = ctx.enter_context(tc.tile_pool(name="staging", bufs=5))
        psum = ctx.enter_context(tc.psum_pool(name="psum", bufs=8))
        ctx.enter_context(tc.manual_schedule())

        w_raw = const.tile([P, 12, CHANNELS], BF16)
        x_raw = [const.tile([P, PACK, POSITIONS], BF16, name="x_raw%d" % b) for b in range(BATCH)]

        def load_w(g):
            nc.sync.dma_start(
                out=w_raw[:, 4 * g : 4 * g + 4, :],
                in_=W_qkv[OUT_COLS * g : OUT_COLS * (g + 1), :].rearrange("(a o) k -> o a k", o=P),
            )

        def load_x(b):
            nc.sync.dma_start(
                out=x_raw[b][:].rearrange("q (u e) n -> q u e n", u=2),
                in_=x[b].rearrange("c h w -> c (h w)").rearrange("(u q e) n -> q u e n", u=2, e=2),
            )

        load_w(0)
        load_x(0)
        load_w(1)
        load_w(2)
        for b in range(1, BATCH):
            load_x(b)

        zero = const.tile([P, 1], F32)
        nc.vector.memset(zero[:], 0.0)
        ten_thousand = const.tile([P, 2], F32)
        nc.vector.memset(ten_thousand[:], 10000.0)
        warm = const.tile([P, 1], F32)
        nc.scalar.activation(out=warm[:], in_=zero[:], func=ACT.Sin)
        half_pi = const.tile([P, 1], F32)
        nc.vector.tensor_scalar(
            out=half_pi[:], in0=zero[:], scalar1=math.pi / 2, scalar2=None, op0=ALU.add
        )

        count = const.tile([P, GROUPS], F32)
        nc.gpsimd.iota(
            count[:], pattern=[[1, GROUPS]], base=0, channel_multiplier=0,
            allow_small_or_imprecise_dtypes=True,
        )
        position = const.tile([P, 2, GROUPS, HALF_RUN], F32)
        for s in range(2):
            nc.vector.scalar_tensor_tensor(
                out=position[:, s, :, :],
                in0=count[:].unsqueeze(2).to_broadcast([P, GROUPS, HALF_RUN]),
                scalar=float(RUN),
                in1=count[:, HALF_RUN * s : HALF_RUN * (s + 1)]
                .unsqueeze(1)
                .to_broadcast([P, GROUPS, HALF_RUN]),
                op0=ALU.mult,
                op1=ALU.add,
            )

        rate_index = const.tile([P, 2], F32)
        nc.gpsimd.iota(
            rate_index[:], pattern=[[1, 2]], base=0, channel_multiplier=2,
            allow_small_or_imprecise_dtypes=True,
        )
        exponent = const.tile([P, 2], F32)
        nc.gpsimd.tensor_scalar(
            out=exponent[:], in0=rate_index[:], scalar1=-1.0 / 256.0, scalar2=0.0,
            op0=ALU.mult, op1=ALU.add,
        )
        rate = const.tile([P, 2], F32)
        nc.gpsimd.tensor_tensor(out=rate[:], in0=ten_thousand[:], in1=exponent[:], op=ALU.pow)

        identity = const.tile([P, P], F32)
        make_identity(nc, identity[:])

        w_grouped = const.tile([P, 3 * OUT_COLS * PACK], BF16, align_bytes=64)
        w_words = w_grouped[:].bitcast(F32).rearrange("q (o u) -> q o u", u=2)
        w_codes = const.tile([P, 3 * OUT_COLS], U32, align_bytes=64)
        w_scales = const.tile([P, 3 * OUT_COLS], U8, align_bytes=64)
        flipped = {}

        def flip_w(g):
            for pair in range(2 * g, 2 * g + 2):
                flipped[pair] = psum.tile([P, 2, 2, P], F32, name="flipped", tag="bank")
                for a in range(2):
                    words = w_raw[:, 2 * pair + a, :].bitcast(F32)
                    for u in range(2):
                        nc.tensor.transpose(
                            flipped[pair][:, a, u, :], words[:, P * u : P * (u + 1)], identity[:]
                        )

        def regroup_w(g):
            for pair in range(2 * g, 2 * g + 2):
                dst = w_words[:, 2 * P * pair : 2 * P * (pair + 1), :].rearrange(
                    "q (a o) u -> q a o u", a=2
                )
                src = flipped[pair][:].rearrange("q a u o -> q a o u")
                if g % 2 == 0:
                    nc.scalar.copy(out=dst, in_=src)
                else:
                    nc.vector.tensor_copy(out=dst, in_=src)

        def quantise_w(g):
            cols = slice(OUT_COLS * g, OUT_COLS * (g + 1))
            nc.vector.quantize_mx(
                out=w_codes[:, cols].bitcast(FP8X4),
                scales=w_scales[:, cols],
                in_=w_grouped[:, PACK * OUT_COLS * g : PACK * OUT_COLS * (g + 1)],
            )

        pe = [const.tile([P, PACK, HALF_COLS], F32, name="pe%d" % s) for s in range(2)]

        def make_table(s, e):
            angle = angles.tile([P, HALF_COLS], F32)
            nc.vector.tensor_scalar(
                out=angle[:], in0=position[:, s, :, :].rearrange("q m t -> q (m t)"),
                scalar1=rate[:, e : e + 1], scalar2=1.0 / (2.0 * math.pi), op0=ALU.mult, op1=ALU.mult,
            )
            whole = angles.tile([P, HALF_COLS], F32)
            nc.vector.tensor_scalar(
                out=whole[:], in0=angle[:], scalar1=ROUND_MAGIC, scalar2=None, op0=ALU.add
            )
            back = angles.tile([P, HALF_COLS], F32)
            nc.vector.scalar_tensor_tensor(
                out=back[:], in0=whole[:], scalar=ROUND_MAGIC, in1=angle[:],
                op0=ALU.subtract, op1=ALU.subtract,
            )
            size = angles.tile([P, HALF_COLS], F32)
            nc.scalar.activation(out=size[:], in_=back[:], func=ACT.Abs)
            nc.scalar.activation(out=pe[s][:, e, :], in_=back[:], func=ACT.Sin, scale=-2.0 * math.pi)
            nc.scalar.activation(
                out=pe[s][:, 2 + e, :], in_=size[:], func=ACT.Sin, scale=-2.0 * math.pi,
                bias=half_pi[:],
            )

        token_tiles = {}

        def add_table(b, s):
            if s == 0:
                token_tiles[b] = (
                    tokens.tile([P, RUN, GROUPS, PACK], BF16, name="grouped", align_bytes=64),
                    tokens.tile([P, RUN, GROUPS], U32, name="codes", align_bytes=64),
                    tokens.tile([P, RUN, GROUPS], U8, name="scales", align_bytes=64),
                )
            grouped = token_tiles[b][0]
            half = slice(HALF_RUN * s, HALF_RUN * (s + 1))
            nc.vector.tensor_tensor(
                out=grouped[:, half, :, :].rearrange("q t m j -> q m j t"),
                in0=x_raw[b][:].rearrange("q j (m s t) -> q s m j t", s=2, t=HALF_RUN)[:, s],
                in1=pe[s][:].rearrange("q j (m t) -> q m j t", t=HALF_RUN),
                op=ALU.add,
            )

        def quantise_tokens(b, s):
            grouped, codes, scales = token_tiles[b]
            half = slice(HALF_RUN * s, HALF_RUN * (s + 1))
            nc.vector.quantize_mx(
                out=codes[:, half, :].rearrange("q t m -> q (t m)").bitcast(FP8X4),
                scales=scales[:, half, :].rearrange("q t m -> q (t m)"),
                in_=grouped[:, half, :, :].rearrange("q t m j -> q (t m j)"),
            )

        def prepare_tokens(b, step):
            if step < 2:
                add_table(b, step)
            if step > 0:
                quantise_tokens(b, step - 1)

        stage_tiles = {}

        def project(b, g, s):
            codes, scales = token_tiles[b][1], token_tiles[b][2]
            cols = slice(OUT_COLS * g, OUT_COLS * (g + 1))
            if s == 0:
                stage_tiles[(b, g)] = staging.tile([P, HEADS, RUN, HEAD_DIM], F32, name="stage")
            stage = stage_tiles[(b, g)]
            for t in range(HALF_RUN * s, HALF_RUN * (s + 1)):
                acc = psum.tile([P, OUT_COLS], F32, tag="bank")
                nc.tensor.matmul_mx(
                    out=acc[:],
                    lhsT=codes[:, t, :].bitcast(FP8X4),
                    lhsT_scale=scales[:, t, :],
                    rhs=w_codes[:, cols].bitcast(FP8X4),
                    rhs_scale=w_scales[:, cols],
                    start=True,
                    stop=True,
                )
                by_head = acc[:].rearrange("m (h d) -> m h d", d=HEAD_DIM)
                if t % 4 == 3:
                    nc.vector.tensor_copy(out=stage[:, :, t, :], in_=by_head)
                else:
                    nc.scalar.copy(out=stage[:, :, t, :], in_=by_head)

        def store(b, g, part, parts):
            nc.sync.dma_start(
                out=outs[g][b].rearrange("h (m c r) d -> c m h (r d)", c=parts, r=RUN // parts)[part],
                in_=stage_tiles[(b, g)][:].rearrange("m h (c r) d -> m c h (r d)", c=parts)[:, part],
            )

        make_table(0, 0)
        make_table(0, 1)
        flip_w(0)
        flip_w(1)
        regroup_w(0)
        make_table(1, 0)
        make_table(1, 1)
        flip_w(2)
        add_table(0, 0)
        quantise_w(0)
        quantise_tokens(0, 0)
        regroup_w(1)
        quantise_w(1)
        project(0, 0, 0)
        store(0, 0, 0, 2)
        regroup_w(2)
        add_table(0, 1)
        quantise_w(2)
        quantise_tokens(0, 1)
        for g in range(1, 3):
            project(0, g, 0)
            store(0, g, 0, 2)
        for g in range(3):
            project(0, g, 1)
            store(0, g, 1, 2)
            prepare_tokens(1, g)

        for b in range(1, BATCH):
            for g in range(3):
                project(b, g, 0)
                project(b, g, 1)
                store(b, g, 0, 1)
                if b + 1 < BATCH:
                    prepare_tokens(b + 1, g)
